import numpy as np
import ml_dtypes


def mxq(x, axis, fmt="e4m3"):
    dtype, down = {"e4m3": (ml_dtypes.float8_e4m3fn, 7), "e5m2": (ml_dtypes.float8_e5m2, 14)}[fmt]
    v = np.moveaxis(np.asarray(x, np.float32).astype(ml_dtypes.bfloat16).astype(np.float64), axis, -1)
    blocks = v.reshape(v.shape[:-1] + (-1, 32))
    amax = np.abs(blocks).max(-1, keepdims=True)
    byte = np.maximum(np.where(amax > 0, np.frexp(amax)[1] - 1 + 127, 0) - down, 1)
    scale = np.exp2(byte - 127.0)
    codes = (blocks / scale).astype(np.float32).astype(dtype).astype(np.float64)
    return np.moveaxis((codes * scale).reshape(v.shape), -1, axis)


WIDE = False


def mx_kscale(k):
    if not WIDE:
        return np.ones(k)
    levels = np.array([10, -10, 5, -5, 0])
    a = np.random.permutation(np.resize(levels, k // 512 * 4)).reshape(k // 512, 4)
    idx = np.arange(k)
    return np.exp2(a[idx // 512, idx % 128 // 32])


BF16 = ml_dtypes.bfloat16


def bf(x):
    return np.asarray(x, np.float32).astype(BF16)


def f64(x):
    return np.asarray(x).astype(np.float64)


B, HEADS, CH, H, W, HSP, WSP = 2, 2, 256, 32, 64, 32, 32
C = HEADS * CH
U, V = H // HSP, W // WSP
NW = U * V
N = HSP * WSP


def _vid2win(x):
    x = x.reshape(B, HEADS, CH, U, HSP, V, WSP)
    x = x.transpose(0, 3, 5, 1, 4, 6, 2)
    return x.reshape(B * NW, HEADS, N, CH)


def setup_inputs():
    s = mx_kscale(N)
    sp = np.tile(s.reshape(HSP, WSP), (U, V))
    kv = np.random.standard_normal((2, B, C, H, W))
    kv[1] = kv[1] / sp * s.max()
    q = np.random.standard_normal((B, C, H, W)) * 1.5
    mask = np.random.standard_normal((NW, N, N)) + np.log(s)[None, None, :]
    return {"kv": bf(kv), "q": bf(q), "mask": bf(mask)}


def reference(kv, q, mask):
    kv = f64(kv)
    k, v = kv[0], kv[1]
    qw = _vid2win(f64(q))
    kw = _vid2win(k)
    vw = _vid2win(v)
    attn = (qw @ kw.transpose(0, 1, 3, 2)) * CH ** (-0.5)
    attn = attn.reshape(B, NW, HEADS, N, N) + f64(mask)[None, :, None]
    attn = attn.reshape(B * NW, HEADS, N, N)
    e = np.exp(attn - attn.max(-1, keepdims=True))
    x = (mxq(e, 3, "e4m3") @ mxq(vw, 2, "e4m3")) / e.sum(-1, keepdims=True)
    x = x.reshape(B, U, V, HEADS, HSP, WSP, CH)
    x = x.transpose(0, 3, 6, 1, 4, 2, 5)
    return x.reshape(B, C, H, W)

@@ -1,0 +1,319 @@
+from contextlib import ExitStack
+
+import concourse.bass as bass
+import concourse.mybir as mybir
+import concourse.tile as tile
+from concourse.masks import make_identity
+
+F32 = mybir.dt.float32
+BF16 = mybir.dt.bfloat16
+U32 = mybir.dt.uint32
+U8 = mybir.dt.uint8
+FP8X4 = mybir.dt.float8_e4m3fn_x4
+ALU = mybir.AluOpType
+ACT = mybir.ActivationFunctionType
+AX = mybir.AxisListType
+
+P = 128
+NKEY = 1024
+NT = 64
+FLOPS = 2 * 2 * 8 * 1024 * 1024 * 256
+
+MANUAL = True
+T_LAG = 3
+
+
+def tile_window_attention_t_kernel(tc, kv, q, mask, out):
+    nc = tc.nc
+    with ExitStack() as ctx:
+        const = ctx.enter_context(tc.tile_pool(name="const", bufs=1))
+        maskp = ctx.enter_context(tc.tile_pool(name="maskp", bufs=1))
+        inp = ctx.enter_context(tc.tile_pool(name="inp", bufs=2))
+        work = ctx.enter_context(tc.tile_pool(name="work", bufs=2))
+        ps_s = ctx.enter_context(tc.psum_pool(name="ps_s", bufs=2))
+        ps_t = ctx.enter_context(tc.psum_pool(name="ps_t", bufs=2))
+        ps_o = ctx.enter_context(tc.psum_pool(name="ps_o", bufs=1))
+        if MANUAL:
+            ctx.enter_context(tc.manual_schedule())
+
+        ident_bf = const.tile([P, P], BF16, name="ident_bf")
+        make_identity(nc, ident_bf[:])
+        ident_f = const.tile([P, P], F32, name="ident_f")
+        make_identity(nc, ident_f[:])
+
+        mask_sb = [maskp.tile([P, 8, NKEY], BF16, name="mask%d" % v) for v in range(2)]
+
+        kraw = {}
+        qd = {}
+        vd = {}
+        oa = {}
+        vcode = {}
+        vscale = {}
+        gvt = {}
+        st = {}
+        ut = {}
+        nmt = {}
+        et = {}
+        xtt = {}
+        grp = {}
+        rst = {}
+        rt = {}
+        rsb = {}
+        ecode = {}
+        escale = {}
+        ot = {}
+
+        def chan0(pr, cc):
+            return (pr % 2) * 256 + cc * P
+
+        def load_k(pr, cc):
+            t = inp.tile([P, 2048], BF16, name="kraw%d" % cc, tag="kraw%d" % cc)
+            kraw[(pr, cc)] = t
+            c0 = chan0(pr, cc)
+            nc.sync.dma_start(out=t[:], in_=kv[0, pr // 2, c0:c0 + P].rearrange("c h w -> c (h w)"))
+
+        def alloc_win(store, label, pr, cc, v):
+            t = inp.tile([P, NKEY], BF16, name="%s%d%d" % (label, cc, v), tag="%s%d%d" % (label, cc, v))
+            store[(pr, cc, v)] = t
+
+        def load_win(store, src, pr, cc, v, h0, h1):
+            c0 = chan0(pr, cc)
+            t = store[(pr, cc, v)]
+            nc.sync.dma_start(
+                out=t[:, h0 * 32:h1 * 32].rearrange("c (h w) -> c h w", w=32),
+                in_=src[c0:c0 + P, h0:h1, v * 32:(v + 1) * 32],
+            )
+
+        def load_mask(v, t0):
+            nc.sync.dma_start(
+                out=mask_sb[v][:, t0:t0 + 2, :],
+                in_=mask[v, t0 * P:(t0 + 2) * P, :].rearrange("(t p) k -> p t k", p=P),
+            )
+
+        def load_pair(pr):
+            b = pr // 2
+            first = pr == 0
+            for cc in range(2):
+                for v in range(2):
+                    alloc_win(qd, "qd", pr, cc, v)
+                    alloc_win(vd, "vd", pr, cc, v)
+            if first:
+                for cc in range(2):
+                    load_win(qd, q[b], pr, cc, 0, 0, 8)
+            for cc in range(2):
+                load_k(pr, cc)
+            if first:
+                load_mask(0, 0)
+                for cc in range(2):
+                    load_win(qd, q[b], pr, cc, 0, 8, 32)
+                load_mask(0, 2)
+            else:
+                for cc in range(2):
+                    load_win(qd, q[b], pr, cc, 0, 0, 32)
+            for cc in range(2):
+                load_win(vd, kv[1, b], pr, cc, 0, 0, 32)
+            if first:
+                load_mask(0, 4)
+                load_mask(0, 6)
+            for cc in range(2):
+                load_win(qd, q[b], pr, cc, 1, 0, 32)
+            if first:
+                load_mask(1, 0)
+                load_mask(1, 2)
+            for cc in range(2):
+                load_win(vd, kv[1, b], pr, cc, 1, 0, 32)
+            if first:
+                load_mask(1, 4)
+                load_mask(1, 6)
+
+        def where(i):
+            inst = i // 8
+            return inst // 2, inst % 2, i % 8
+
+        def qk_ops(i):
+            pr, v, qt = where(i)
+            s0 = ps_s.tile([P, 512], F32, name="s0", tag="s0")
+            s1 = ps_s.tile([P, 512], F32, name="s1", tag="s1")
+            st[i] = (s0, s1)
+            ops = []
+            for cc in range(2):
+                for nh in range(2):
+                    ops.append((i, cc, nh))
+            return ops
+
+        def qk_mm(i, cc, nh):
+            pr, v, qt = where(i)
+            kview = kraw[(pr, cc)][:].rearrange("c (h v w) -> c h v w", v=2, w=32)
+            nc.tensor.matmul(
+                out=st[i][nh][:].rearrange("p (h w) -> p h w", w=32),
+                lhsT=qd[(pr, cc, v)][:, qt * P:(qt + 1) * P],
+                rhs=kview[:, nh * 16:(nh + 1) * 16, v, :],
+                start=(cc == 0),
+                stop=(cc == 1),
+            )
+
+        def tr_alloc(i):
+            xtt[i] = ps_t.tile([P, 8, P], BF16, name="xt", tag="t")
+
+        def tr_one(i, kb):
+            nc.tensor.transpose(out=xtt[i][:, kb, :], in_=et[i][:, kb * P:(kb + 1) * P], identity=ident_bf[:])
+
+        def pe_step(s):
+            mms = qk_ops(s) if s < NT else []
+            j = s - T_LAG
+            trs = list(range(8)) if 0 <= j < NT else []
+            if trs:
+                tr_alloc(j)
+            for n in range(4):
+                if mms:
+                    qk_mm(*mms[n])
+                for kb in trs[2 * n:2 * n + 2]:
+                    tr_one(j, kb)
+
+        def add_mask_and_max(i):
+            pr, v, qt = where(i)
+            u = work.tile([P, NKEY], F32, name="u", tag="u", bufs=3)
+            ut[i] = u
+            for nh in range(2):
+                nc.vector.scalar_tensor_tensor(
+                    out=u[:, nh * 512:(nh + 1) * 512],
+                    in0=st[i][nh][:],
+                    scalar=-1.0 / 16.0,
+                    in1=mask_sb[v][:, qt, nh * 512:(nh + 1) * 512],
+                    op0=ALU.mult,
+                    op1=ALU.subtract,
+                )
+            nm = work.tile([P, 1], F32, name="nm", tag="nm", bufs=4)
+            nmt[i] = nm
+            nc.vector.tensor_reduce(out=nm[:], in_=u[:], axis=AX.X, op=ALU.min)
+
+        def exp_tile(i):
+            h = i // 4
+            if i % 4 == 0:
+                rst[h] = work.tile([P, 4], F32, name="rs", tag="rs", bufs=3)
+            e = work.tile([P, NKEY], BF16, name="e", tag="e", bufs=4)
+            et[i] = e
+            nc.scalar.activation(
+                out=e[:], in_=ut[i][:], func=ACT.Exp, bias=nmt[i][:], scale=-1.0,
+                accum_out=rst[h][:, i % 4:i % 4 + 1],
+            )
+
+        def evac_tile(i):
+            h = i // 4
+            jj = i % 4
+            if jj == 0:
+                grp[h] = work.tile([P, 2, 512, 4], BF16, name="grp", tag="grp", bufs=2, align_bytes=64)
+            nc.scalar.copy(
+                out=grp[h][:, :, jj * P:(jj + 1) * P, :],
+                in_=xtt[i][:].rearrange("p (g t) n -> p g n t", t=4),
+            )
+
+        def vpath_pe(inst):
+            pr, v = inst // 2, inst % 2
+            gvt[inst] = work.tile([P, 2, 256, 4], BF16, name="gv", tag="gv", bufs=2, align_bytes=64)
+            for cc in range(2):
+                vt = ps_t.tile([P, 8, P], BF16, name="vt", tag="t")
+                for kb in range(8):
+                    nc.tensor.transpose(out=vt[:, kb, :], in_=vd[(pr, cc, v)][:, kb * P:(kb + 1) * P], identity=ident_bf[:])
+                nc.scalar.copy(
+                    out=gvt[inst][:, :, cc * P:(cc + 1) * P, :],
+                    in_=vt[:].rearrange("p (g t) c -> p g c t", t=4),
+                )
+
+        def vpath_q(inst):
+            vcode[inst] = work.tile([P, 512], U32, name="vcode", tag="vcode", bufs=2, align_bytes=64)
+            vscale[inst] = work.tile([P, 512], U8, name="vscale", tag="vscale", bufs=2, align_bytes=64)
+            nc.vector.quantize_mx(
+                out=vcode[inst][:].bitcast(FP8X4),
+                scales=vscale[inst][:],
+                in_=gvt[inst][:].rearrange("p g c t -> p (g c t)"),
+            )
+
+        def recip(h):
+            rt[h] = work.tile([P, 4], F32, name="r", tag="r", bufs=3)
+            nc.vector.reciprocal(out=rt[h][:], in_=rst[h][:])
+
+        def quant_e(h):
+            ecode[h] = work.tile([P, 1024], U32, name="ecode", tag="ecode", bufs=2, align_bytes=64)
+            escale[h] = work.tile([P, 1024], U8, name="escale", tag="escale", bufs=2, align_bytes=64)
+            nc.vector.quantize_mx(
+                out=ecode[h][:].bitcast(FP8X4),
+                scales=escale[h][:],
+                in_=grp[h][:].rearrange("p g n t -> p (g n t)"),
+            )
+
+        def spread_r(h):
+            rp = ps_t.tile([P, 512], F32, name="rp", tag="t")
+            for jj in range(4):
+                nc.tensor.transpose(
+                    out=rp[:, jj * P:(jj + 1) * P],
+                    in_=rt[h][:, jj:jj + 1].to_broadcast([P, P]),
+                    identity=ident_f[:],
+                )
+            rsb[h] = work.tile([P, 512], F32, name="rsb", tag="rsb", bufs=2)
+            nc.scalar.copy(out=rsb[h][:], in_=rp[:])
+
+        def mx(h):
+            inst = h // 2
+            o0 = ps_o.tile([P, 512], F32, name="o0", tag="o0")
+            o1 = ps_o.tile([P, 512], F32, name="o1", tag="o1")
+            ot[h] = (o0, o1)
+            for cc in range(2):
+                for g in range(2):
+                    w0 = g * 256 + cc * P
+                    nc.tensor.matmul_mx(
+                        out=ot[h][cc][:],
+                        lhsT=vcode[inst][:, w0:w0 + P].bitcast(FP8X4),
+                        lhsT_scale=vscale[inst][:, w0:w0 + P],
+                        rhs=ecode[h][:, g * 512:(g + 1) * 512].bitcast(FP8X4),
+                        rhs_scale=escale[h][:, g * 512:(g + 1) * 512],
+                        start=(g == 0),
+                        stop=(g == 1),
+                    )
+
+        def norm_store(h):
+            inst = h // 2
+            pr, v, hf = inst // 2, inst % 2, h % 2
+            if v == 0 and hf == 0:
+                for cc in range(2):
+                    oa[(pr, cc)] = work.tile([P, 32, 2, 32], F32, name="oa%d" % cc, tag="oa%d" % cc, bufs=2)
+            for cc in range(2):
+                nc.vector.tensor_tensor(
+                    out=oa[(pr, cc)][:, hf * 16:(hf + 1) * 16, v, :],
+                    in0=ot[h][cc][:].rearrange("p (h w) -> p h w", w=32),
+                    in1=rsb[h][:].rearrange("p (h w) -> p h w", w=32),
+                    op=ALU.mult,
+                )
+            if v == 1:
+                for cc in range(2):
+                    c0 = chan0(pr, cc)
+                    nc.gpsimd.dma_start(
+                        out=out[pr // 2, c0:c0 + P, hf * 16:(hf + 1) * 16, :].rearrange("c h w -> c (h w)"),
+                        in_=oa[(pr, cc)][:, hf * 16:(hf + 1) * 16, :, :].rearrange("c h v w -> c (h v w)"),
+                    )
+
+        load_pair(0)
+        for s in range(NT + 12):
+            if s % 16 == 0 and s // 16 + 1 < 4:
+                load_pair(s // 16 + 1)
+            pe_step(s)
+            if 0 <= s - T_LAG < NT:
+                evac_tile(s - T_LAG)
+            if s % 8 == 3 and s < NT:
+                vpath_pe(s // 8)
+            if s >= 8 and (s - 8) % 4 == 0 and (s - 8) // 4 < 16:
+                spread_r((s - 8) // 4)
+            if s >= 9 and (s - 9) % 4 == 0 and (s - 9) // 4 < 16:
+                mx((s - 9) // 4)
+            if 0 <= s - 1 < NT:
+                exp_tile(s - 1)
+            if s < NT:
+                add_mask_and_max(s)
+            if s % 8 == 4 and s < NT:
+                vpath_q(s // 8)
+            if s >= 6 and (s - 6) % 4 == 0 and (s - 6) // 4 < 16:
+                recip((s - 6) // 4)
+            if s >= 7 and (s - 7) % 4 == 0 and (s - 7) // 4 < 16:
+                quant_e((s - 7) // 4)
+            if s >= 11 and (s - 11) % 4 == 0 and (s - 11) // 4 < 16:
+                norm_store((s - 11) // 4)

@@ -1,8 +1,6 @@
 from contextlib import ExitStack
 
-import concourse.bass as bass
 import concourse.mybir as mybir
-import concourse.tile as tile
 from concourse.masks import make_identity
 
 F32 = mybir.dt.float32
@@ -20,7 +18,9 @@ NT = 64
 FLOPS = 2 * 2 * 8 * 1024 * 1024 * 256
 
 MANUAL = True
-T_LAG = 3
+T_LAG = 5
+PE_MASK = (2, 7, 12)
+LAST_SPLIT = (2, 1, 1)
 
 
 def tile_window_attention_t_kernel(tc, kv, q, mask, out):
@@ -40,8 +40,23 @@ def tile_window_attention_t_kernel(tc, kv, q, mask, out):
         make_identity(nc, ident_bf[:])
         ident_f = const.tile([P, P], F32, name="ident_f")
         make_identity(nc, ident_f[:])
+        ident16 = const.tile([P, P], BF16, name="ident16")
+        nc.vector.tensor_scalar_mul(out=ident16[:], in0=ident_bf[:], scalar1=16.0)
 
         mask_sb = [maskp.tile([P, 8, NKEY], BF16, name="mask%d" % v) for v in range(2)]
+
+        groups = [(4 * h, 4) for h in range(15)]
+        first = 60
+        for n in LAST_SPLIT:
+            groups.append((first, n))
+            first += n
+        group_of = {}
+        for gi, (g0, gn) in enumerate(groups):
+            for i in range(g0, g0 + gn):
+                group_of[i] = gi
+        by_last = {}
+        for gi, (g0, gn) in enumerate(groups):
+            by_last[g0 + gn - 1] = gi
 
         kraw = {}
         qd = {}
@@ -66,11 +81,15 @@ def tile_window_attention_t_kernel(tc, kv, q, mask, out):
         def chan0(pr, cc):
             return (pr % 2) * 256 + cc * P
 
-        def load_k(pr, cc):
-            t = inp.tile([P, 2048], BF16, name="kraw%d" % cc, tag="kraw%d" % cc)
-            kraw[(pr, cc)] = t
+        def alloc_k(pr, cc):
+            kraw[(pr, cc)] = inp.tile([P, 2048], BF16, name="kraw%d" % cc, tag="kraw%d" % cc)
+
+        def load_k(pr, cc, h0, h1):
             c0 = chan0(pr, cc)
-            nc.sync.dma_start(out=t[:], in_=kv[0, pr // 2, c0:c0 + P].rearrange("c h w -> c (h w)"))
+            nc.sync.dma_start(
+                out=kraw[(pr, cc)][:, h0 * 64:h1 * 64],
+                in_=kv[0, pr // 2, c0:c0 + P, h0:h1, :].rearrange("c h w -> c (h w)"),
+            )
 
         def alloc_win(store, label, pr, cc, v):
             t = inp.tile([P, NKEY], BF16, name="%s%d%d" % (label, cc, v), tag="%s%d%d" % (label, cc, v))
@@ -84,127 +103,145 @@ def tile_window_attention_t_kernel(tc, kv, q, mask, out):
                 in_=src[c0:c0 + P, h0:h1, v * 32:(v + 1) * 32],
             )
 
-        def load_mask(v, t0):
+        def load_mask(v, t0, n):
             nc.sync.dma_start(
-                out=mask_sb[v][:, t0:t0 + 2, :],
-                in_=mask[v, t0 * P:(t0 + 2) * P, :].rearrange("(t p) k -> p t k", p=P),
+                out=mask_sb[v][:, t0:t0 + n, :],
+                in_=mask[v, t0 * P:(t0 + n) * P, :].rearrange("(t p) k -> p t k", p=P),
             )
 
         def load_pair(pr):
             b = pr // 2
-            first = pr == 0
             for cc in range(2):
+                alloc_k(pr, cc)
                 for v in range(2):
                     alloc_win(qd, "qd", pr, cc, v)
                     alloc_win(vd, "vd", pr, cc, v)
-            if first:
+            if pr == 0:
                 for cc in range(2):
-                    load_win(qd, q[b], pr, cc, 0, 0, 8)
-            for cc in range(2):
-                load_k(pr, cc)
-            if first:
-                load_mask(0, 0)
+                    load_win(qd, q[b], pr, cc, 0, 0, 4)
                 for cc in range(2):
-                    load_win(qd, q[b], pr, cc, 0, 8, 32)
-                load_mask(0, 2)
+                    load_k(pr, cc, 0, 16)
+                load_mask(0, 0, 1)
+                for cc in range(2):
+                    load_k(pr, cc, 16, 32)
+                for cc in range(2):
+                    load_win(qd, q[b], pr, cc, 0, 4, 16)
+                load_mask(0, 1, 1)
+                load_mask(0, 2, 2)
+                for cc in range(2):
+                    load_win(qd, q[b], pr, cc, 0, 16, 32)
+                load_mask(0, 4, 4)
+                for cc in range(2):
+                    load_win(vd, kv[1, b], pr, cc, 0, 0, 32)
+                for cc in range(2):
+                    load_win(qd, q[b], pr, cc, 1, 0, 32)
+                load_mask(1, 0, 4)
+                for cc in range(2):
+                    load_win(vd, kv[1, b], pr, cc, 1, 0, 32)
+                load_mask(1, 4, 4)
             else:
                 for cc in range(2):
-                    load_win(qd, q[b], pr, cc, 0, 0, 32)
-            for cc in range(2):
-                load_win(vd, kv[1, b], pr, cc, 0, 0, 32)
-            if first:
-                load_mask(0, 4)
-                load_mask(0, 6)
-            for cc in range(2):
-                load_win(qd, q[b], pr, cc, 1, 0, 32)
-            if first:
-                load_mask(1, 0)
-                load_mask(1, 2)
-            for cc in range(2):
-                load_win(vd, kv[1, b], pr, cc, 1, 0, 32)
-            if first:
-                load_mask(1, 4)
-                load_mask(1, 6)
+                    load_k(pr, cc, 0, 32)
+                for v in range(2):
+                    for cc in range(2):
+                        load_win(qd, q[b], pr, cc, v, 0, 32)
+                    for cc in range(2):
+                        load_win(vd, kv[1, b], pr, cc, v, 0, 32)
 
         def where(i):
             inst = i // 8
             return inst // 2, inst % 2, i % 8
 
-        def qk_ops(i):
+        def on_pe(i):
+            return i % 16 in PE_MASK
+
+        def scores(i):
             pr, v, qt = where(i)
             s0 = ps_s.tile([P, 512], F32, name="s0", tag="s0")
             s1 = ps_s.tile([P, 512], F32, name="s1", tag="s1")
             st[i] = (s0, s1)
-            ops = []
             for cc in range(2):
+                kview = kraw[(pr, cc)][:].rearrange("c (h v w) -> c h v w", v=2, w=32)
                 for nh in range(2):
-                    ops.append((i, cc, nh))
-            return ops
+                    nc.tensor.matmul(
+                        out=st[i][nh][:].rearrange("p (h w) -> p h w", w=32),
+                        lhsT=qd[(pr, cc, v)][:, qt * P:(qt + 1) * P],
+                        rhs=kview[:, nh * 16:(nh + 1) * 16, v, :],
+                        start=(cc == 0),
+                        stop=(cc == 1 and not on_pe(i)),
+                    )
+            if on_pe(i):
+                for nh in range(2):
+                    nc.tensor.matmul(
+                        out=st[i][nh][:],
+                        lhsT=ident16[:],
+                        rhs=mask_sb[v][:, qt, nh * 512:(nh + 1) * 512],
+                        start=False,
+                        stop=True,
+                    )
 
-        def qk_mm(i, cc, nh):
-            pr, v, qt = where(i)
-            kview = kraw[(pr, cc)][:].rearrange("c (h v w) -> c h v w", v=2, w=32)
-            nc.tensor.matmul(
-                out=st[i][nh][:].rearrange("p (h w) -> p h w", w=32),
-                lhsT=qd[(pr, cc, v)][:, qt * P:(qt + 1) * P],
-                rhs=kview[:, nh * 16:(nh + 1) * 16, v, :],
-                start=(cc == 0),
-                stop=(cc == 1),
-            )
-
-        def tr_alloc(i):
+        def transposes(i):
             xtt[i] = ps_t.tile([P, 8, P], BF16, name="xt", tag="t")
+            for kb in range(8):
+                nc.tensor.transpose(out=xtt[i][:, kb, :], in_=et[i][:, kb * P:(kb + 1) * P], identity=ident_bf[:])
 
-        def tr_one(i, kb):
-            nc.tensor.transpose(out=xtt[i][:, kb, :], in_=et[i][:, kb * P:(kb + 1) * P], identity=ident_bf[:])
+        nm2t = {}
 
-        def pe_step(s):
-            mms = qk_ops(s) if s < NT else []
-            j = s - T_LAG
-            trs = list(range(8)) if 0 <= j < NT else []
-            if trs:
-                tr_alloc(j)
-            for n in range(4):
-                if mms:
-                    qk_mm(*mms[n])
-                for kb in trs[2 * n:2 * n + 2]:
-                    tr_one(j, kb)
-
-        def add_mask_and_max(i):
+        def leave_psum(i):
             pr, v, qt = where(i)
-            u = work.tile([P, NKEY], F32, name="u", tag="u", bufs=3)
+            u = work.tile([P, NKEY], F32, name="u", tag="u", bufs=4)
             ut[i] = u
+            if on_pe(i):
+                nm2t[i] = work.tile([P, 2], F32, name="nm2", tag="nm2", bufs=2)
             for nh in range(2):
-                nc.vector.scalar_tensor_tensor(
-                    out=u[:, nh * 512:(nh + 1) * 512],
-                    in0=st[i][nh][:],
-                    scalar=-1.0 / 16.0,
-                    in1=mask_sb[v][:, qt, nh * 512:(nh + 1) * 512],
-                    op0=ALU.mult,
-                    op1=ALU.subtract,
-                )
-            nm = work.tile([P, 1], F32, name="nm", tag="nm", bufs=4)
+                if on_pe(i):
+                    nc.vector.tensor_scalar(
+                        out=u[:, nh * 512:(nh + 1) * 512],
+                        in0=st[i][nh][:],
+                        scalar1=-1.0 / 16.0,
+                        scalar2=None,
+                        op0=ALU.mult,
+                        op1=ALU.min,
+                        accum_out=nm2t[i][:, nh:nh + 1],
+                    )
+                else:
+                    nc.vector.scalar_tensor_tensor(
+                        out=u[:, nh * 512:(nh + 1) * 512],
+                        in0=st[i][nh][:],
+                        scalar=-1.0 / 16.0,
+                        in1=mask_sb[v][:, qt, nh * 512:(nh + 1) * 512],
+                        op0=ALU.mult,
+                        op1=ALU.subtract,
+                    )
+
+        def row_min(i):
+            nm = work.tile([P, 1], F32, name="nm", tag="nm", bufs=5)
             nmt[i] = nm
-            nc.vector.tensor_reduce(out=nm[:], in_=u[:], axis=AX.X, op=ALU.min)
+            if on_pe(i):
+                nc.vector.tensor_tensor(out=nm[:], in0=nm2t[i][:, 0:1], in1=nm2t[i][:, 1:2], op=ALU.min)
+            else:
+                nc.vector.tensor_reduce(out=nm[:], in_=ut[i][:], axis=AX.X, op=ALU.min)
 
         def exp_tile(i):
-            h = i // 4
-            if i % 4 == 0:
-                rst[h] = work.tile([P, 4], F32, name="rs", tag="rs", bufs=3)
-            e = work.tile([P, NKEY], BF16, name="e", tag="e", bufs=4)
+            gi = group_of[i]
+            g0, gn = groups[gi]
+            if i == g0:
+                rst[gi] = work.tile([P, 4], F32, name="rs", tag="rs", bufs=4)
+            e = work.tile([P, NKEY], BF16, name="e", tag="e", bufs=T_LAG)
             et[i] = e
             nc.scalar.activation(
                 out=e[:], in_=ut[i][:], func=ACT.Exp, bias=nmt[i][:], scale=-1.0,
-                accum_out=rst[h][:, i % 4:i % 4 + 1],
+                accum_out=rst[gi][:, i - g0:i - g0 + 1],
             )
 
         def evac_tile(i):
-            h = i // 4
-            jj = i % 4
+            gi = group_of[i]
+            g0, gn = groups[gi]
+            jj = i - g0
             if jj == 0:
-                grp[h] = work.tile([P, 2, 512, 4], BF16, name="grp", tag="grp", bufs=2, align_bytes=64)
+                grp[gi] = work.tile([P, 2, gn * P, 4], BF16, name="grp", tag="grp", bufs=2, align_bytes=64)
             nc.scalar.copy(
-                out=grp[h][:, :, jj * P:(jj + 1) * P, :],
+                out=grp[gi][:, :, jj * P:(jj + 1) * P, :],
                 in_=xtt[i][:].rearrange("p (g t) n -> p g n t", t=4),
             )
 
@@ -229,91 +266,101 @@ def tile_window_attention_t_kernel(tc, kv, q, mask, out):
                 in_=gvt[inst][:].rearrange("p g c t -> p (g c t)"),
             )
 
-        def recip(h):
-            rt[h] = work.tile([P, 4], F32, name="r", tag="r", bufs=3)
-            nc.vector.reciprocal(out=rt[h][:], in_=rst[h][:])
+        def recip(gi):
+            g0, gn = groups[gi]
+            rt[gi] = work.tile([P, 4], F32, name="r", tag="r", bufs=3)
+            nc.vector.reciprocal(out=rt[gi][:, 0:gn], in_=rst[gi][:, 0:gn])
 
-        def quant_e(h):
-            ecode[h] = work.tile([P, 1024], U32, name="ecode", tag="ecode", bufs=2, align_bytes=64)
-            escale[h] = work.tile([P, 1024], U8, name="escale", tag="escale", bufs=2, align_bytes=64)
+        def quant_e(gi):
+            g0, gn = groups[gi]
+            ecode[gi] = work.tile([P, 2 * gn * P], U32, name="ecode", tag="ecode", bufs=2, align_bytes=64)
+            escale[gi] = work.tile([P, 2 * gn * P], U8, name="escale", tag="escale", bufs=2, align_bytes=64)
             nc.vector.quantize_mx(
-                out=ecode[h][:].bitcast(FP8X4),
-                scales=escale[h][:],
-                in_=grp[h][:].rearrange("p g n t -> p (g n t)"),
+                out=ecode[gi][:].bitcast(FP8X4),
+                scales=escale[gi][:],
+                in_=grp[gi][:].rearrange("p g n t -> p (g n t)"),
             )
 
-        def spread_r(h):
-            rp = ps_t.tile([P, 512], F32, name="rp", tag="t")
-            for jj in range(4):
+        def spread_r(gi):
+            g0, gn = groups[gi]
+            rp = ps_t.tile([P, gn * P], F32, name="rp", tag="t")
+            for jj in range(gn):
                 nc.tensor.transpose(
                     out=rp[:, jj * P:(jj + 1) * P],
-                    in_=rt[h][:, jj:jj + 1].to_broadcast([P, P]),
+                    in_=rt[gi][:, jj:jj + 1].to_broadcast([P, P]),
                     identity=ident_f[:],
                 )
-            rsb[h] = work.tile([P, 512], F32, name="rsb", tag="rsb", bufs=2)
-            nc.scalar.copy(out=rsb[h][:], in_=rp[:])
+            rsb[gi] = work.tile([P, gn * P], F32, name="rsb", tag="rsb", bufs=2)
+            nc.scalar.copy(out=rsb[gi][:], in_=rp[:])
 
-        def mx(h):
-            inst = h // 2
-            o0 = ps_o.tile([P, 512], F32, name="o0", tag="o0")
-            o1 = ps_o.tile([P, 512], F32, name="o1", tag="o1")
-            ot[h] = (o0, o1)
+        def mx(gi):
+            g0, gn = groups[gi]
+            inst = g0 // 8
+            w = gn * P
+            o0 = ps_o.tile([P, w], F32, name="o0", tag="o0")
+            o1 = ps_o.tile([P, w], F32, name="o1", tag="o1")
+            ot[gi] = (o0, o1)
             for cc in range(2):
                 for g in range(2):
                     w0 = g * 256 + cc * P
                     nc.tensor.matmul_mx(
-                        out=ot[h][cc][:],
+                        out=ot[gi][cc][:],
                         lhsT=vcode[inst][:, w0:w0 + P].bitcast(FP8X4),
                         lhsT_scale=vscale[inst][:, w0:w0 + P],
-                        rhs=ecode[h][:, g * 512:(g + 1) * 512].bitcast(FP8X4),
-                        rhs_scale=escale[h][:, g * 512:(g + 1) * 512],
+                        rhs=ecode[gi][:, g * w:(g + 1) * w].bitcast(FP8X4),
+                        rhs_scale=escale[gi][:, g * w:(g + 1) * w],
                         start=(g == 0),
                         stop=(g == 1),
                     )
 
-        def norm_store(h):
-            inst = h // 2
-            pr, v, hf = inst // 2, inst % 2, h % 2
-            if v == 0 and hf == 0:
+        def norm_store(gi):
+            g0, gn = groups[gi]
+            pr, v, qt = where(g0)
+            h0, h1 = qt * 4, (qt + gn) * 4
+            if v == 0 and qt == 0:
                 for cc in range(2):
                     oa[(pr, cc)] = work.tile([P, 32, 2, 32], F32, name="oa%d" % cc, tag="oa%d" % cc, bufs=2)
             for cc in range(2):
                 nc.vector.tensor_tensor(
-                    out=oa[(pr, cc)][:, hf * 16:(hf + 1) * 16, v, :],
-                    in0=ot[h][cc][:].rearrange("p (h w) -> p h w", w=32),
-                    in1=rsb[h][:].rearrange("p (h w) -> p h w", w=32),
+                    out=oa[(pr, cc)][:, h0:h1, v, :],
+                    in0=ot[gi][cc][:].rearrange("p (h w) -> p h w", w=32),
+                    in1=rsb[gi][:].rearrange("p (h w) -> p h w", w=32),
                     op=ALU.mult,
                 )
             if v == 1:
                 for cc in range(2):
                     c0 = chan0(pr, cc)
-                    nc.gpsimd.dma_start(
-                        out=out[pr // 2, c0:c0 + P, hf * 16:(hf + 1) * 16, :].rearrange("c h w -> c (h w)"),
-                        in_=oa[(pr, cc)][:, hf * 16:(hf + 1) * 16, :, :].rearrange("c h v w -> c (h v w)"),
+                    nc.sync.dma_start(
+                        out=out[pr // 2, c0:c0 + P, h0:h1, :].rearrange("c h w -> c (h w)"),
+                        in_=oa[(pr, cc)][:, h0:h1, :, :].rearrange("c h v w -> c (h v w)"),
                     )
 
         load_pair(0)
-        for s in range(NT + 12):
+        for s in range(NT + T_LAG + 8):
             if s % 16 == 0 and s // 16 + 1 < 4:
                 load_pair(s // 16 + 1)
-            pe_step(s)
-            if 0 <= s - T_LAG < NT:
-                evac_tile(s - T_LAG)
-            if s % 8 == 3 and s < NT:
-                vpath_pe(s // 8)
-            if s >= 8 and (s - 8) % 4 == 0 and (s - 8) // 4 < 16:
-                spread_r((s - 8) // 4)
-            if s >= 9 and (s - 9) % 4 == 0 and (s - 9) // 4 < 16:
-                mx((s - 9) // 4)
-            if 0 <= s - 1 < NT:
-                exp_tile(s - 1)
+            if s - T_LAG - 3 in by_last:
+                norm_store(by_last[s - T_LAG - 3])
             if s < NT:
-                add_mask_and_max(s)
-            if s % 8 == 4 and s < NT:
-                vpath_q(s // 8)
-            if s >= 6 and (s - 6) % 4 == 0 and (s - 6) // 4 < 16:
-                recip((s - 6) // 4)
-            if s >= 7 and (s - 7) % 4 == 0 and (s - 7) // 4 < 16:
-                quant_e((s - 7) // 4)
-            if s >= 11 and (s - 11) % 4 == 0 and (s - 11) // 4 < 16:
-                norm_store((s - 11) // 4)
+                scores(s)
+            if s - T_LAG - 2 in by_last:
+                mx(by_last[s - T_LAG - 2])
+            if 0 <= s - T_LAG < NT:
+                transposes(s - T_LAG)
+                evac_tile(s - T_LAG)
+            if s % 8 == 6 and s < NT:
+                vpath_pe(s // 8)
+            if s - T_LAG - 1 in by_last:
+                spread_r(by_last[s - T_LAG - 1])
+            if 0 <= s - 2 < NT:
+                exp_tile(s - 2)
+            if s < NT:
+                leave_psum(s)
+            if 0 <= s - 1 < NT:
+                row_min(s - 1)
+            if s % 8 == 0 and 1 <= s // 8 <= 8:
+                vpath_q(s // 8 - 1)
+            if s - 4 in by_last:
+                recip(by_last[s - 4])
+            if s - T_LAG - 1 in by_last:
+                quant_e(by_last[s - T_LAG - 1])

@@ -155,64 +155,62 @@ def tile_window_attention_t_kernel(tc, kv, q, mask, out):
         def on_pe(i):
             return i % 16 in PE_MASK
 
-        def scores(i):
+        def scores(i, nh):
             pr, v, qt = where(i)
-            s0 = ps_s.tile([P, 512], F32, name="s0", tag="s0")
-            s1 = ps_s.tile([P, 512], F32, name="s1", tag="s1")
-            st[i] = (s0, s1)
+            s_nh = ps_s.tile([P, 512], F32, name="s%d" % nh, tag="s%d" % nh)
+            st[(i, nh)] = s_nh
             for cc in range(2):
                 kview = kraw[(pr, cc)][:].rearrange("c (h v w) -> c h v w", v=2, w=32)
-                for nh in range(2):
-                    nc.tensor.matmul(
-                        out=st[i][nh][:].rearrange("p (h w) -> p h w", w=32),
-                        lhsT=qd[(pr, cc, v)][:, qt * P:(qt + 1) * P],
-                        rhs=kview[:, nh * 16:(nh + 1) * 16, v, :],
-                        start=(cc == 0),
-                        stop=(cc == 1 and not on_pe(i)),
-                    )
+                nc.tensor.matmul(
+                    out=s_nh[:].rearrange("p (h w) -> p h w", w=32),
+                    lhsT=qd[(pr, cc, v)][:, qt * P:(qt + 1) * P],
+                    rhs=kview[:, nh * 16:(nh + 1) * 16, v, :],
+                    start=(cc == 0),
+                    stop=(cc == 1 and not on_pe(i)),
+                )
             if on_pe(i):
-                for nh in range(2):
-                    nc.tensor.matmul(
-                        out=st[i][nh][:],
-                        lhsT=ident16[:],
-                        rhs=mask_sb[v][:, qt, nh * 512:(nh + 1) * 512],
-                        start=False,
-                        stop=True,
-                    )
+                nc.tensor.matmul(
+                    out=s_nh[:],
+                    lhsT=ident16[:],
+                    rhs=mask_sb[v][:, qt, nh * 512:(nh + 1) * 512],
+                    start=False,
+                    stop=True,
+                )
 
-        def transposes(i):
-            xtt[i] = ps_t.tile([P, 8, P], BF16, name="xt", tag="t")
-            for kb in range(8):
+        def transposes(i, part):
+            if part == 0:
+                xtt[i] = ps_t.tile([P, 8, P], BF16, name="xt", tag="t")
+            for kb in range(4 * part, 4 * part + 4):
                 nc.tensor.transpose(out=xtt[i][:, kb, :], in_=et[i][:, kb * P:(kb + 1) * P], identity=ident_bf[:])
 
         nm2t = {}
 
-        def leave_psum(i):
+        def leave_psum(i, nh):
             pr, v, qt = where(i)
-            u = work.tile([P, NKEY], F32, name="u", tag="u", bufs=4)
-            ut[i] = u
-            if on_pe(i):
-                nm2t[i] = work.tile([P, 2], F32, name="nm2", tag="nm2", bufs=2)
-            for nh in range(2):
+            if nh == 0:
+                ut[i] = work.tile([P, NKEY], F32, name="u", tag="u", bufs=4)
                 if on_pe(i):
-                    nc.vector.tensor_scalar(
-                        out=u[:, nh * 512:(nh + 1) * 512],
-                        in0=st[i][nh][:],
-                        scalar1=-1.0 / 16.0,
-                        scalar2=None,
-                        op0=ALU.mult,
-                        op1=ALU.min,
-                        accum_out=nm2t[i][:, nh:nh + 1],
-                    )
-                else:
-                    nc.vector.scalar_tensor_tensor(
-                        out=u[:, nh * 512:(nh + 1) * 512],
-                        in0=st[i][nh][:],
-                        scalar=-1.0 / 16.0,
-                        in1=mask_sb[v][:, qt, nh * 512:(nh + 1) * 512],
-                        op0=ALU.mult,
-                        op1=ALU.subtract,
-                    )
+                    nm2t[i] = work.tile([P, 2], F32, name="nm2", tag="nm2", bufs=2)
+            u = ut[i]
+            if on_pe(i):
+                nc.vector.tensor_scalar(
+                    out=u[:, nh * 512:(nh + 1) * 512],
+                    in0=st[(i, nh)][:],
+                    scalar1=-1.0 / 16.0,
+                    scalar2=None,
+                    op0=ALU.mult,
+                    op1=ALU.min,
+                    accum_out=nm2t[i][:, nh:nh + 1],
+                )
+            else:
+                nc.vector.scalar_tensor_tensor(
+                    out=u[:, nh * 512:(nh + 1) * 512],
+                    in0=st[(i, nh)][:],
+                    scalar=-1.0 / 16.0,
+                    in1=mask_sb[v][:, qt, nh * 512:(nh + 1) * 512],
+                    op0=ALU.mult,
+                    op1=ALU.subtract,
+                )
 
         def row_min(i):
             nm = work.tile([P, 1], F32, name="nm", tag="nm", bufs=5)
@@ -290,7 +288,7 @@ def tile_window_attention_t_kernel(tc, kv, q, mask, out):
                     in_=rt[gi][:, jj:jj + 1].to_broadcast([P, P]),
                     identity=ident_f[:],
                 )
-            rsb[gi] = work.tile([P, gn * P], F32, name="rsb", tag="rsb", bufs=2)
+            rsb[gi] = work.tile([P, gn * P], F32, name="rsb", tag="rsb", bufs=3)
             nc.scalar.copy(out=rsb[gi][:], in_=rp[:])
 
         def mx(gi):
@@ -313,54 +311,69 @@ def tile_window_attention_t_kernel(tc, kv, q, mask, out):
                         stop=(g == 1),
                     )
 
-        def norm_store(gi):
+        def norm_store(gi, cc):
             g0, gn = groups[gi]
             pr, v, qt = where(g0)
             h0, h1 = qt * 4, (qt + gn) * 4
             if v == 0 and qt == 0:
-                for cc in range(2):
-                    oa[(pr, cc)] = work.tile([P, 32, 2, 32], F32, name="oa%d" % cc, tag="oa%d" % cc, bufs=2)
-            for cc in range(2):
-                nc.vector.tensor_tensor(
-                    out=oa[(pr, cc)][:, h0:h1, v, :],
-                    in0=ot[gi][cc][:].rearrange("p (h w) -> p h w", w=32),
-                    in1=rsb[gi][:].rearrange("p (h w) -> p h w", w=32),
-                    op=ALU.mult,
-                )
+                oa[(pr, cc)] = work.tile([P, 32, 2, 32], F32, name="oa%d" % cc, tag="oa%d" % cc, bufs=2)
+            nc.vector.tensor_tensor(
+                out=oa[(pr, cc)][:, h0:h1, v, :],
+                in0=ot[gi][cc][:].rearrange("p (h w) -> p h w", w=32),
+                in1=rsb[gi][:].rearrange("p (h w) -> p h w", w=32),
+                op=ALU.mult,
+            )
             if v == 1:
-                for cc in range(2):
-                    c0 = chan0(pr, cc)
-                    nc.sync.dma_start(
-                        out=out[pr // 2, c0:c0 + P, h0:h1, :].rearrange("c h w -> c (h w)"),
-                        in_=oa[(pr, cc)][:, h0:h1, :, :].rearrange("c h v w -> c (h v w)"),
-                    )
+                c0 = chan0(pr, cc)
+                nc.sync.dma_start(
+                    out=out[pr // 2, c0:c0 + P, h0:h1, :].rearrange("c h w -> c (h w)"),
+                    in_=oa[(pr, cc)][:, h0:h1, :, :].rearrange("c h v w -> c (h v w)"),
+                )
+
+        vpe_at = {6: 0}
+        vq_at = {8: 0}
+        for inst in range(1, 8):
+            vpe_at[8 * inst + 4] = inst
+            vq_at[8 * inst + 6] = inst
 
         load_pair(0)
         for s in range(NT + T_LAG + 8):
             if s % 16 == 0 and s // 16 + 1 < 4:
                 load_pair(s // 16 + 1)
-            if s - T_LAG - 3 in by_last:
-                norm_store(by_last[s - T_LAG - 3])
+            j = s - T_LAG
             if s < NT:
-                scores(s)
-            if s - T_LAG - 2 in by_last:
-                mx(by_last[s - T_LAG - 2])
-            if 0 <= s - T_LAG < NT:
-                transposes(s - T_LAG)
-                evac_tile(s - T_LAG)
-            if s % 8 == 6 and s < NT:
-                vpath_pe(s // 8)
-            if s - T_LAG - 1 in by_last:
-                spread_r(by_last[s - T_LAG - 1])
+                scores(s, 0)
+            if 0 <= j < NT:
+                transposes(j, 0)
+            if s < NT:
+                scores(s, 1)
+            if j - 3 in by_last:
+                mx(by_last[j - 3])
+            if 0 <= j < NT:
+                transposes(j, 1)
+                evac_tile(j)
+            if s in vpe_at:
+                vpath_pe(vpe_at[s])
+            if j - 1 in by_last:
+                spread_r(by_last[j - 1])
             if 0 <= s - 2 < NT:
                 exp_tile(s - 2)
             if s < NT:
-                leave_psum(s)
+                leave_psum(s, 0)
             if 0 <= s - 1 < NT:
                 row_min(s - 1)
-            if s % 8 == 0 and 1 <= s // 8 <= 8:
-                vpath_q(s // 8 - 1)
+            if s < NT:
+                leave_psum(s, 1)
+            if s in vq_at:
+                vpath_q(vq_at[s])
             if s - 4 in by_last:
                 recip(by_last[s - 4])
-            if s - T_LAG - 1 in by_last:
-                quant_e(by_last[s - T_LAG - 1])
+            if j - 1 in by_last:
+                quant_e(by_last[j - 1])
+            if j - 3 in by_last:
+                gi = by_last[j - 3]
+                norm_store(gi, 0)
+                if groups[gi][0] >= 60:
+                    norm_store(gi, 1)
+            if j - 4 in by_last and groups[by_last[j - 4]][0] < 60:
+                norm_store(by_last[j - 4], 1)

@@ -20,6 +20,8 @@ FLOPS = 2 * 2 * 8 * 1024 * 1024 * 256
 MANUAL = True
 T_LAG = 5
 PE_MASK = (2, 7, 12)
+GP_TILES = 3
+GP_NORM = (1,)
 LAST_SPLIT = (2, 1, 1)
 
 
@@ -238,10 +240,19 @@ def tile_window_attention_t_kernel(tc, kv, q, mask, out):
             jj = i - g0
             if jj == 0:
                 grp[gi] = work.tile([P, 2, gn * P, 4], BF16, name="grp", tag="grp", bufs=2, align_bytes=64)
-            nc.scalar.copy(
-                out=grp[gi][:, :, jj * P:(jj + 1) * P, :],
-                in_=xtt[i][:].rearrange("p (g t) n -> p g n t", t=4),
-            )
+            if gn == 4 and jj < GP_TILES:
+                xs = work.tile([P, 8, P], BF16, name="xs", tag="xs", bufs=3)
+                nc.scalar.copy(out=xs[:], in_=xtt[i][:])
+                nc.gpsimd.tensor_scalar(
+                    out=grp[gi][:, :, jj * P:(jj + 1) * P, :],
+                    in0=xs[:].rearrange("p (g t) n -> p g n t", t=4),
+                    scalar1=1.0, scalar2=0.0, op0=ALU.mult, op1=ALU.add,
+                )
+            else:
+                nc.scalar.copy(
+                    out=grp[gi][:, :, jj * P:(jj + 1) * P, :],
+                    in_=xtt[i][:].rearrange("p (g t) n -> p g n t", t=4),
+                )
 
         def vpath_pe(inst):
             pr, v = inst // 2, inst % 2
@@ -250,9 +261,12 @@ def tile_window_attention_t_kernel(tc, kv, q, mask, out):
                 vt = ps_t.tile([P, 8, P], BF16, name="vt", tag="t")
                 for kb in range(8):
                     nc.tensor.transpose(out=vt[:, kb, :], in_=vd[(pr, cc, v)][:, kb * P:(kb + 1) * P], identity=ident_bf[:])
-                nc.scalar.copy(
+                xv = work.tile([P, 8, P], BF16, name="xv", tag="xs", bufs=3)
+                nc.scalar.copy(out=xv[:], in_=vt[:])
+                nc.gpsimd.tensor_scalar(
                     out=gvt[inst][:, :, cc * P:(cc + 1) * P, :],
-                    in_=vt[:].rearrange("p (g t) c -> p g c t", t=4),
+                    in0=xv[:].rearrange("p (g t) c -> p g c t", t=4),
+                    scalar1=1.0, scalar2=0.0, op0=ALU.mult, op1=ALU.add,
                 )
 
         def vpath_q(inst):
@@ -317,12 +331,22 @@ def tile_window_attention_t_kernel(tc, kv, q, mask, out):
             h0, h1 = qt * 4, (qt + gn) * 4
             if v == 0 and qt == 0:
                 oa[(pr, cc)] = work.tile([P, 32, 2, 32], F32, name="oa%d" % cc, tag="oa%d" % cc, bufs=2)
-            nc.vector.tensor_tensor(
-                out=oa[(pr, cc)][:, h0:h1, v, :],
-                in0=ot[gi][cc][:].rearrange("p (h w) -> p h w", w=32),
-                in1=rsb[gi][:].rearrange("p (h w) -> p h w", w=32),
-                op=ALU.mult,
-            )
+            if gn == 4 and cc in GP_NORM:
+                osb = work.tile([P, 512], F32, name="osb", tag="osb", bufs=2)
+                nc.scalar.copy(out=osb[:], in_=ot[gi][cc][:])
+                nc.gpsimd.tensor_tensor(
+                    out=oa[(pr, cc)][:, h0:h1, v, :],
+                    in0=osb[:].rearrange("p (h w) -> p h w", w=32),
+                    in1=rsb[gi][:].rearrange("p (h w) -> p h w", w=32),
+                    op=ALU.mult,
+                )
+            else:
+                nc.vector.tensor_tensor(
+                    out=oa[(pr, cc)][:, h0:h1, v, :],
+                    in0=ot[gi][cc][:].rearrange("p (h w) -> p h w", w=32),
+                    in1=rsb[gi][:].rearrange("p (h w) -> p h w", w=32),
+                    op=ALU.mult,
+                )
             if v == 1:
                 c0 = chan0(pr, cc)
                 nc.sync.dma_start(
@@ -356,6 +380,8 @@ def tile_window_attention_t_kernel(tc, kv, q, mask, out):
                 vpath_pe(vpe_at[s])
             if j - 1 in by_last:
                 spread_r(by_last[j - 1])
+            if j - 4 in by_last and groups[by_last[j - 4]][0] < 60:
+                norm_store(by_last[j - 4], 1)
             if 0 <= s - 2 < NT:
                 exp_tile(s - 2)
             if s < NT:
@@ -375,5 +401,3 @@ def tile_window_attention_t_kernel(tc, kv, q, mask, out):
                 norm_store(gi, 0)
                 if groups[gi][0] >= 60:
                     norm_store(gi, 1)
-            if j - 4 in by_last and groups[by_last[j - 4]][0] < 60:
-                norm_store(by_last[j - 4], 1)

@@ -20,8 +20,7 @@ FLOPS = 2 * 2 * 8 * 1024 * 1024 * 256
 MANUAL = True
 T_LAG = 5
 PE_MASK = (2, 7, 12)
-GP_TILES = 3
-GP_NORM = (1,)
+EVAC_V = (21, 45, 60, 61, 62)
 LAST_SPLIT = (2, 1, 1)
 
 
@@ -240,19 +239,15 @@ def tile_window_attention_t_kernel(tc, kv, q, mask, out):
             jj = i - g0
             if jj == 0:
                 grp[gi] = work.tile([P, 2, gn * P, 4], BF16, name="grp", tag="grp", bufs=2, align_bytes=64)
-            if gn == 4 and jj < GP_TILES:
-                xs = work.tile([P, 8, P], BF16, name="xs", tag="xs", bufs=3)
-                nc.scalar.copy(out=xs[:], in_=xtt[i][:])
-                nc.gpsimd.tensor_scalar(
-                    out=grp[gi][:, :, jj * P:(jj + 1) * P, :],
-                    in0=xs[:].rearrange("p (g t) n -> p g n t", t=4),
-                    scalar1=1.0, scalar2=0.0, op0=ALU.mult, op1=ALU.add,
-                )
+            dst = grp[gi][:, :, jj * P:(jj + 1) * P, :]
+            src = xtt[i][:].rearrange("p (g t) n -> p g n t", t=4)
+            if i == NT - 1:
+                nc.scalar.copy(out=dst[:, 0, :, :], in_=src[:, 0, :, :])
+                nc.vector.tensor_copy(out=dst[:, 1, :, :], in_=src[:, 1, :, :])
+            elif i in EVAC_V:
+                nc.vector.tensor_copy(out=dst, in_=src)
             else:
-                nc.scalar.copy(
-                    out=grp[gi][:, :, jj * P:(jj + 1) * P, :],
-                    in_=xtt[i][:].rearrange("p (g t) n -> p g n t", t=4),
-                )
+                nc.scalar.copy(out=dst, in_=src)
 
         def vpath_pe(inst):
             pr, v = inst // 2, inst % 2
@@ -261,12 +256,9 @@ def tile_window_attention_t_kernel(tc, kv, q, mask, out):
                 vt = ps_t.tile([P, 8, P], BF16, name="vt", tag="t")
                 for kb in range(8):
                     nc.tensor.transpose(out=vt[:, kb, :], in_=vd[(pr, cc, v)][:, kb * P:(kb + 1) * P], identity=ident_bf[:])
-                xv = work.tile([P, 8, P], BF16, name="xv", tag="xs", bufs=3)
-                nc.scalar.copy(out=xv[:], in_=vt[:])
-                nc.gpsimd.tensor_scalar(
+                nc.scalar.copy(
                     out=gvt[inst][:, :, cc * P:(cc + 1) * P, :],
-                    in0=xv[:].rearrange("p (g t) c -> p g c t", t=4),
-                    scalar1=1.0, scalar2=0.0, op0=ALU.mult, op1=ALU.add,
+                    in_=vt[:].rearrange("p (g t) c -> p g c t", t=4),
                 )
 
         def vpath_q(inst):
@@ -331,22 +323,12 @@ def tile_window_attention_t_kernel(tc, kv, q, mask, out):
             h0, h1 = qt * 4, (qt + gn) * 4
             if v == 0 and qt == 0:
                 oa[(pr, cc)] = work.tile([P, 32, 2, 32], F32, name="oa%d" % cc, tag="oa%d" % cc, bufs=2)
-            if gn == 4 and cc in GP_NORM:
-                osb = work.tile([P, 512], F32, name="osb", tag="osb", bufs=2)
-                nc.scalar.copy(out=osb[:], in_=ot[gi][cc][:])
-                nc.gpsimd.tensor_tensor(
-                    out=oa[(pr, cc)][:, h0:h1, v, :],
-                    in0=osb[:].rearrange("p (h w) -> p h w", w=32),
-                    in1=rsb[gi][:].rearrange("p (h w) -> p h w", w=32),
-                    op=ALU.mult,
-                )
-            else:
-                nc.vector.tensor_tensor(
-                    out=oa[(pr, cc)][:, h0:h1, v, :],
-                    in0=ot[gi][cc][:].rearrange("p (h w) -> p h w", w=32),
-                    in1=rsb[gi][:].rearrange("p (h w) -> p h w", w=32),
-                    op=ALU.mult,
-                )
+            nc.vector.tensor_tensor(
+                out=oa[(pr, cc)][:, h0:h1, v, :],
+                in0=ot[gi][cc][:].rearrange("p (h w) -> p h w", w=32),
+                in1=rsb[gi][:].rearrange("p (h w) -> p h w", w=32),
+                op=ALU.mult,
+            )
             if v == 1:
                 c0 = chan0(pr, cc)
                 nc.sync.dma_start(
@@ -375,21 +357,24 @@ def tile_window_attention_t_kernel(tc, kv, q, mask, out):
                 mx(by_last[j - 3])
             if 0 <= j < NT:
                 transposes(j, 1)
-                evac_tile(j)
+                if j not in EVAC_V:
+                    evac_tile(j)
             if s in vpe_at:
                 vpath_pe(vpe_at[s])
             if j - 1 in by_last:
                 spread_r(by_last[j - 1])
-            if j - 4 in by_last and groups[by_last[j - 4]][0] < 60:
-                norm_store(by_last[j - 4], 1)
             if 0 <= s - 2 < NT:
                 exp_tile(s - 2)
             if s < NT:
                 leave_psum(s, 0)
-            if 0 <= s - 1 < NT:
+            if 1 <= s - 1 < NT:
                 row_min(s - 1)
             if s < NT:
                 leave_psum(s, 1)
+            if s == 0:
+                row_min(0)
+            if j in EVAC_V:
+                evac_tile(j)
             if s in vq_at:
                 vpath_q(vq_at[s])
             if s - 4 in by_last:
@@ -401,3 +386,5 @@ def tile_window_attention_t_kernel(tc, kv, q, mask, out):
                 norm_store(gi, 0)
                 if groups[gi][0] >= 60:
                     norm_store(gi, 1)
+            if j - 4 in by_last and groups[by_last[j - 4]][0] < 60:
+                norm_store(by_last[j - 4], 1)

@@ -19,8 +19,7 @@ FLOPS = 2 * 2 * 8 * 1024 * 1024 * 256
 
 MANUAL = True
 T_LAG = 5
-PE_MASK = (2, 7, 12)
-EVAC_V = (21, 45, 60, 61, 62)
+PE_MASK = (2, 7, 12, 18, 23, 28, 34, 39, 44, 50, 55, 63)
 LAST_SPLIT = (2, 1, 1)
 
 
@@ -154,7 +153,7 @@ def tile_window_attention_t_kernel(tc, kv, q, mask, out):
             return inst // 2, inst % 2, i % 8
 
         def on_pe(i):
-            return i % 16 in PE_MASK
+            return i in PE_MASK
 
         def scores(i, nh):
             pr, v, qt = where(i)
@@ -191,17 +190,18 @@ def tile_window_attention_t_kernel(tc, kv, q, mask, out):
             if nh == 0:
                 ut[i] = work.tile([P, NKEY], F32, name="u", tag="u", bufs=4)
                 if on_pe(i):
-                    nm2t[i] = work.tile([P, 2], F32, name="nm2", tag="nm2", bufs=2)
+                    nm2t[i] = work.tile([P, 1], F32, name="nm2", tag="nm2", bufs=2)
+                    nmt[i] = work.tile([P, 1], F32, name="nm", tag="nm", bufs=5)
             u = ut[i]
             if on_pe(i):
                 nc.vector.tensor_scalar(
                     out=u[:, nh * 512:(nh + 1) * 512],
                     in0=st[(i, nh)][:],
                     scalar1=-1.0 / 16.0,
-                    scalar2=None,
+                    scalar2=(None if nh == 0 else nm2t[i][:]),
                     op0=ALU.mult,
                     op1=ALU.min,
-                    accum_out=nm2t[i][:, nh:nh + 1],
+                    accum_out=(nm2t[i][:] if nh == 0 else nmt[i][:]),
                 )
             else:
                 nc.vector.scalar_tensor_tensor(
@@ -214,11 +214,9 @@ def tile_window_attention_t_kernel(tc, kv, q, mask, out):
                 )
 
         def row_min(i):
-            nm = work.tile([P, 1], F32, name="nm", tag="nm", bufs=5)
-            nmt[i] = nm
-            if on_pe(i):
-                nc.vector.tensor_tensor(out=nm[:], in0=nm2t[i][:, 0:1], in1=nm2t[i][:, 1:2], op=ALU.min)
-            else:
+            if not on_pe(i):
+                nm = work.tile([P, 1], F32, name="nm", tag="nm", bufs=5)
+                nmt[i] = nm
                 nc.vector.tensor_reduce(out=nm[:], in_=ut[i][:], axis=AX.X, op=ALU.min)
 
         def exp_tile(i):
@@ -239,15 +237,10 @@ def tile_window_attention_t_kernel(tc, kv, q, mask, out):
             jj = i - g0
             if jj == 0:
                 grp[gi] = work.tile([P, 2, gn * P, 4], BF16, name="grp", tag="grp", bufs=2, align_bytes=64)
-            dst = grp[gi][:, :, jj * P:(jj + 1) * P, :]
-            src = xtt[i][:].rearrange("p (g t) n -> p g n t", t=4)
-            if i == NT - 1:
-                nc.scalar.copy(out=dst[:, 0, :, :], in_=src[:, 0, :, :])
-                nc.vector.tensor_copy(out=dst[:, 1, :, :], in_=src[:, 1, :, :])
-            elif i in EVAC_V:
-                nc.vector.tensor_copy(out=dst, in_=src)
-            else:
-                nc.scalar.copy(out=dst, in_=src)
+            nc.scalar.copy(
+                out=grp[gi][:, :, jj * P:(jj + 1) * P, :],
+                in_=xtt[i][:].rearrange("p (g t) n -> p g n t", t=4),
+            )
 
         def vpath_pe(inst):
             pr, v = inst // 2, inst % 2
@@ -357,8 +350,7 @@ def tile_window_attention_t_kernel(tc, kv, q, mask, out):
                 mx(by_last[j - 3])
             if 0 <= j < NT:
                 transposes(j, 1)
-                if j not in EVAC_V:
-                    evac_tile(j)
+                evac_tile(j)
             if s in vpe_at:
                 vpath_pe(vpe_at[s])
             if j - 1 in by_last:
@@ -373,8 +365,6 @@ def tile_window_attention_t_kernel(tc, kv, q, mask, out):
                 leave_psum(s, 1)
             if s == 0:
                 row_min(0)
-            if j in EVAC_V:
-                evac_tile(j)
             if s in vq_at:
                 vpath_q(vq_at[s])
             if s - 4 in by_last:

from contextlib import ExitStack

import concourse.mybir as mybir
from concourse.masks import make_identity

F32 = mybir.dt.float32
BF16 = mybir.dt.bfloat16
U32 = mybir.dt.uint32
U8 = mybir.dt.uint8
FP8X4 = mybir.dt.float8_e4m3fn_x4
ALU = mybir.AluOpType
ACT = mybir.ActivationFunctionType
AX = mybir.AxisListType

P = 128
NKEY = 1024
NT = 64
FLOPS = 2 * 2 * 8 * 1024 * 1024 * 256

MANUAL = True
T_LAG = 5
PE_MASK = (2, 7, 12, 18, 23, 28, 34, 39, 44, 50, 55, 63)
LAST_SPLIT = (2, 1, 1)


def tile_window_attention_t_kernel(tc, kv, q, mask, out):
    nc = tc.nc
    with ExitStack() as ctx:
        const = ctx.enter_context(tc.tile_pool(name="const", bufs=1))
        maskp = ctx.enter_context(tc.tile_pool(name="maskp", bufs=1))
        inp = ctx.enter_context(tc.tile_pool(name="inp", bufs=2))
        work = ctx.enter_context(tc.tile_pool(name="work", bufs=2))
        ps_s = ctx.enter_context(tc.psum_pool(name="ps_s", bufs=2))
        ps_t = ctx.enter_context(tc.psum_pool(name="ps_t", bufs=2))
        ps_o = ctx.enter_context(tc.psum_pool(name="ps_o", bufs=1))
        if MANUAL:
            ctx.enter_context(tc.manual_schedule())

        ident_bf = const.tile([P, P], BF16, name="ident_bf")
        make_identity(nc, ident_bf[:])
        ident_f = const.tile([P, P], F32, name="ident_f")
        make_identity(nc, ident_f[:])
        ident16 = const.tile([P, P], BF16, name="ident16")
        nc.vector.tensor_scalar_mul(out=ident16[:], in0=ident_bf[:], scalar1=16.0)

        mask_sb = [maskp.tile([P, 8, NKEY], BF16, name="mask%d" % v) for v in range(2)]

        groups = [(4 * h, 4) for h in range(15)]
        first = 60
        for n in LAST_SPLIT:
            groups.append((first, n))
            first += n
        group_of = {}
        for gi, (g0, gn) in enumerate(groups):
            for i in range(g0, g0 + gn):
                group_of[i] = gi
        by_last = {}
        for gi, (g0, gn) in enumerate(groups):
            by_last[g0 + gn - 1] = gi

        kraw = {}
        qd = {}
        vd = {}
        oa = {}
        vcode = {}
        vscale = {}
        gvt = {}
        st = {}
        ut = {}
        nmt = {}
        et = {}
        xtt = {}
        grp = {}
        rst = {}
        rt = {}
        rsb = {}
        ecode = {}
        escale = {}
        ot = {}

        def chan0(pr, cc):
            return (pr % 2) * 256 + cc * P

        def alloc_k(pr, cc):
            kraw[(pr, cc)] = inp.tile([P, 2048], BF16, name="kraw%d" % cc, tag="kraw%d" % cc)

        def load_k(pr, cc, h0, h1):
            c0 = chan0(pr, cc)
            nc.sync.dma_start(
                out=kraw[(pr, cc)][:, h0 * 64:h1 * 64],
                in_=kv[0, pr // 2, c0:c0 + P, h0:h1, :].rearrange("c h w -> c (h w)"),
            )

        def alloc_win(store, label, pr, cc, v):
            t = inp.tile([P, NKEY], BF16, name="%s%d%d" % (label, cc, v), tag="%s%d%d" % (label, cc, v))
            store[(pr, cc, v)] = t

        def load_win(store, src, pr, cc, v, h0, h1):
            c0 = chan0(pr, cc)
            t = store[(pr, cc, v)]
            nc.sync.dma_start(
                out=t[:, h0 * 32:h1 * 32].rearrange("c (h w) -> c h w", w=32),
                in_=src[c0:c0 + P, h0:h1, v * 32:(v + 1) * 32],
            )

        def load_mask(v, t0, n):
            nc.sync.dma_start(
                out=mask_sb[v][:, t0:t0 + n, :],
                in_=mask[v, t0 * P:(t0 + n) * P, :].rearrange("(t p) k -> p t k", p=P),
            )

        def load_pair(pr):
            b = pr // 2
            for cc in range(2):
                alloc_k(pr, cc)
                for v in range(2):
                    alloc_win(qd, "qd", pr, cc, v)
                    alloc_win(vd, "vd", pr, cc, v)
            if pr == 0:
                for cc in range(2):
                    load_win(qd, q[b], pr, cc, 0, 0, 4)
                for cc in range(2):
                    load_k(pr, cc, 0, 16)
                load_mask(0, 0, 1)
                for cc in range(2):
                    load_k(pr, cc, 16, 32)
                for cc in range(2):
                    load_win(qd, q[b], pr, cc, 0, 4, 16)
                load_mask(0, 1, 1)
                load_mask(0, 2, 2)
                for cc in range(2):
                    load_win(qd, q[b], pr, cc, 0, 16, 32)
                load_mask(0, 4, 4)
                for cc in range(2):
                    load_win(vd, kv[1, b], pr, cc, 0, 0, 32)
                for cc in range(2):
                    load_win(qd, q[b], pr, cc, 1, 0, 32)
                load_mask(1, 0, 4)
                for cc in range(2):
                    load_win(vd, kv[1, b], pr, cc, 1, 0, 32)
                load_mask(1, 4, 4)
            else:
                for cc in range(2):
                    load_k(pr, cc, 0, 32)
                for v in range(2):
                    for cc in range(2):
                        load_win(qd, q[b], pr, cc, v, 0, 32)
                    for cc in range(2):
                        load_win(vd, kv[1, b], pr, cc, v, 0, 32)

        def where(i):
            inst = i // 8
            return inst // 2, inst % 2, i % 8

        def on_pe(i):
            return i in PE_MASK

        def scores(i, nh):
            pr, v, qt = where(i)
            s_nh = ps_s.tile([P, 512], F32, name="s%d" % nh, tag="s%d" % nh)
            st[(i, nh)] = s_nh
            for cc in range(2):
                kview = kraw[(pr, cc)][:].rearrange("c (h v w) -> c h v w", v=2, w=32)
                nc.tensor.matmul(
                    out=s_nh[:].rearrange("p (h w) -> p h w", w=32),
                    lhsT=qd[(pr, cc, v)][:, qt * P:(qt + 1) * P],
                    rhs=kview[:, nh * 16:(nh + 1) * 16, v, :],
                    start=(cc == 0),
                    stop=(cc == 1 and not on_pe(i)),
                )
            if on_pe(i):
                nc.tensor.matmul(
                    out=s_nh[:],
                    lhsT=ident16[:],
                    rhs=mask_sb[v][:, qt, nh * 512:(nh + 1) * 512],
                    start=False,
                    stop=True,
                )

        def transposes(i, part):
            if part == 0:
                xtt[i] = ps_t.tile([P, 8, P], BF16, name="xt", tag="t")
            for kb in range(4 * part, 4 * part + 4):
                nc.tensor.transpose(out=xtt[i][:, kb, :], in_=et[i][:, kb * P:(kb + 1) * P], identity=ident_bf[:])

        nm2t = {}

        def leave_psum(i, nh):
            pr, v, qt = where(i)
            if nh == 0:
                ut[i] = work.tile([P, NKEY], F32, name="u", tag="u", bufs=4)
                if on_pe(i):
                    nm2t[i] = work.tile([P, 1], F32, name="nm2", tag="nm2", bufs=2)
                    nmt[i] = work.tile([P, 1], F32, name="nm", tag="nm", bufs=5)
            u = ut[i]
            if on_pe(i):
                nc.vector.tensor_scalar(
                    out=u[:, nh * 512:(nh + 1) * 512],
                    in0=st[(i, nh)][:],
                    scalar1=-1.0 / 16.0,
                    scalar2=(None if nh == 0 else nm2t[i][:]),
                    op0=ALU.mult,
                    op1=ALU.min,
                    accum_out=(nm2t[i][:] if nh == 0 else nmt[i][:]),
                )
            else:
                nc.vector.scalar_tensor_tensor(
                    out=u[:, nh * 512:(nh + 1) * 512],
                    in0=st[(i, nh)][:],
                    scalar=-1.0 / 16.0,
                    in1=mask_sb[v][:, qt, nh * 512:(nh + 1) * 512],
                    op0=ALU.mult,
                    op1=ALU.subtract,
                )

        def row_min(i):
            if not on_pe(i):
                nm = work.tile([P, 1], F32, name="nm", tag="nm", bufs=5)
                nmt[i] = nm
                nc.vector.tensor_reduce(out=nm[:], in_=ut[i][:], axis=AX.X, op=ALU.min)

        def exp_tile(i):
            gi = group_of[i]
            g0, gn = groups[gi]
            if i == g0:
                rst[gi] = work.tile([P, 4], F32, name="rs", tag="rs", bufs=4)
            e = work.tile([P, NKEY], BF16, name="e", tag="e", bufs=T_LAG)
            et[i] = e
            nc.scalar.activation(
                out=e[:], in_=ut[i][:], func=ACT.Exp, bias=nmt[i][:], scale=-1.0,
                accum_out=rst[gi][:, i - g0:i - g0 + 1],
            )

        def evac_tile(i):
            gi = group_of[i]
            g0, gn = groups[gi]
            jj = i - g0
            if jj == 0:
                grp[gi] = work.tile([P, 2, gn * P, 4], BF16, name="grp", tag="grp", bufs=2, align_bytes=64)
            nc.scalar.copy(
                out=grp[gi][:, :, jj * P:(jj + 1) * P, :],
                in_=xtt[i][:].rearrange("p (g t) n -> p g n t", t=4),
            )

        def vpath_pe(inst):
            pr, v = inst // 2, inst % 2
            gvt[inst] = work.tile([P, 2, 256, 4], BF16, name="gv", tag="gv", bufs=2, align_bytes=64)
            for cc in range(2):
                vt = ps_t.tile([P, 8, P], BF16, name="vt", tag="t")
                for kb in range(8):
                    nc.tensor.transpose(out=vt[:, kb, :], in_=vd[(pr, cc, v)][:, kb * P:(kb + 1) * P], identity=ident_bf[:])
                nc.scalar.copy(
                    out=gvt[inst][:, :, cc * P:(cc + 1) * P, :],
                    in_=vt[:].rearrange("p (g t) c -> p g c t", t=4),
                )

        def vpath_q(inst):
            vcode[inst] = work.tile([P, 512], U32, name="vcode", tag="vcode", bufs=2, align_bytes=64)
            vscale[inst] = work.tile([P, 512], U8, name="vscale", tag="vscale", bufs=2, align_bytes=64)
            nc.vector.quantize_mx(
                out=vcode[inst][:].bitcast(FP8X4),
                scales=vscale[inst][:],
                in_=gvt[inst][:].rearrange("p g c t -> p (g c t)"),
            )

        def recip(gi):
            g0, gn = groups[gi]
            rt[gi] = work.tile([P, 4], F32, name="r", tag="r", bufs=3)
            nc.vector.reciprocal(out=rt[gi][:, 0:gn], in_=rst[gi][:, 0:gn])

        def quant_e(gi):
            g0, gn = groups[gi]
            ecode[gi] = work.tile([P, 2 * gn * P], U32, name="ecode", tag="ecode", bufs=2, align_bytes=64)
            escale[gi] = work.tile([P, 2 * gn * P], U8, name="escale", tag="escale", bufs=2, align_bytes=64)
            nc.vector.quantize_mx(
                out=ecode[gi][:].bitcast(FP8X4),
                scales=escale[gi][:],
                in_=grp[gi][:].rearrange("p g n t -> p (g n t)"),
            )

        def spread_r(gi):
            g0, gn = groups[gi]
            rp = ps_t.tile([P, gn * P], F32, name="rp", tag="t")
            for jj in range(gn):
                nc.tensor.transpose(
                    out=rp[:, jj * P:(jj + 1) * P],
                    in_=rt[gi][:, jj:jj + 1].to_broadcast([P, P]),
                    identity=ident_f[:],
                )
            rsb[gi] = work.tile([P, gn * P], F32, name="rsb", tag="rsb", bufs=3)
            nc.scalar.copy(out=rsb[gi][:], in_=rp[:])

        def mx(gi):
            g0, gn = groups[gi]
            inst = g0 // 8
            w = gn * P
            o0 = ps_o.tile([P, w], F32, name="o0", tag="o0")
            o1 = ps_o.tile([P, w], F32, name="o1", tag="o1")
            ot[gi] = (o0, o1)
            for cc in range(2):
                for g in range(2):
                    w0 = g * 256 + cc * P
                    nc.tensor.matmul_mx(
                        out=ot[gi][cc][:],
                        lhsT=vcode[inst][:, w0:w0 + P].bitcast(FP8X4),
                        lhsT_scale=vscale[inst][:, w0:w0 + P],
                        rhs=ecode[gi][:, g * w:(g + 1) * w].bitcast(FP8X4),
                        rhs_scale=escale[gi][:, g * w:(g + 1) * w],
                        start=(g == 0),
                        stop=(g == 1),
                    )

        def norm_store(gi, cc):
            g0, gn = groups[gi]
            pr, v, qt = where(g0)
            h0, h1 = qt * 4, (qt + gn) * 4
            if v == 0 and qt == 0:
                oa[(pr, cc)] = work.tile([P, 32, 2, 32], F32, name="oa%d" % cc, tag="oa%d" % cc, bufs=2)
            nc.vector.tensor_tensor(
                out=oa[(pr, cc)][:, h0:h1, v, :],
                in0=ot[gi][cc][:].rearrange("p (h w) -> p h w", w=32),
                in1=rsb[gi][:].rearrange("p (h w) -> p h w", w=32),
                op=ALU.mult,
            )
            if v == 1:
                c0 = chan0(pr, cc)
                nc.sync.dma_start(
                    out=out[pr // 2, c0:c0 + P, h0:h1, :].rearrange("c h w -> c (h w)"),
                    in_=oa[(pr, cc)][:, h0:h1, :, :].rearrange("c h v w -> c (h v w)"),
                )

        vpe_at = {6: 0}
        vq_at = {8: 0}
        for inst in range(1, 8):
            vpe_at[8 * inst + 4] = inst
            vq_at[8 * inst + 6] = inst

        load_pair(0)
        for s in range(NT + T_LAG + 8):
            if s % 16 == 0 and s // 16 + 1 < 4:
                load_pair(s // 16 + 1)
            j = s - T_LAG
            if s < NT:
                scores(s, 0)
            if 0 <= j < NT:
                transposes(j, 0)
            if s < NT:
                scores(s, 1)
            if j - 3 in by_last:
                mx(by_last[j - 3])
            if 0 <= j < NT:
                transposes(j, 1)
                evac_tile(j)
            if s in vpe_at:
                vpath_pe(vpe_at[s])
            if j - 1 in by_last:
                spread_r(by_last[j - 1])
            if 0 <= s - 2 < NT:
                exp_tile(s - 2)
            if s < NT:
                leave_psum(s, 0)
            if 1 <= s - 1 < NT:
                row_min(s - 1)
            if s < NT:
                leave_psum(s, 1)
            if s == 0:
                row_min(0)
            if s in vq_at:
                vpath_q(vq_at[s])
            if s - 4 in by_last:
                recip(by_last[s - 4])
            if j - 1 in by_last:
                quant_e(by_last[j - 1])
            if j - 3 in by_last:
                gi = by_last[j - 3]
                norm_store(gi, 0)
                if groups[gi][0] >= 60:
                    norm_store(gi, 1)
            if j - 4 in by_last and groups[by_last[j - 4]][0] < 60:
                norm_store(by_last[j - 4], 1)
